import numpy as np
import ml_dtypes

BF16 = ml_dtypes.bfloat16


def bf(x):
    return np.asarray(x, np.float32).astype(BF16)


def f32(x):
    return np.asarray(x, np.float32)


def f64(x):
    return np.asarray(x).astype(np.float64)


def striped(idx):
    return np.tile(idx.reshape(-1, 16).T, (8, 1))


F, C, S, N = 128, 128, 256, 128
SIGMA = 2.0


def setup_inputs():
    spread = 0.5 + np.random.random((1, N))
    emb = bf(0.5 + spread * np.random.standard_normal((F, N)))
    base = f32(np.random.random((C, S)))
    return {"emb": emb, "base": base, "offs": striped(np.random.permutation(S)[:N])}


def reference(emb, base, offs):
    idx = offs[:16].T.reshape(-1)
    e = f64(emb)
    mu = np.sum(e) / e.size
    var = np.sum((e - mu) ** 2) / (e.size - 1)
    sq = np.sum(e * e, axis=0)
    inner = e.T @ e
    d2 = np.maximum((sq[:, None] + sq[None, :] - 2.0 * inner) / (F * var), 0.0)
    res = f64(base).copy()
    res[:, idx] = np.exp(-d2 / SIGMA)
    return res

@@ -1,0 +1,61 @@
+import concourse.mybir as mybir
+
+F = 128
+N = 128
+S = 256
+COUNT = F * N
+
+FLOPS = 2 * F * N * N
+
+BF16, F32, U16 = mybir.dt.bfloat16, mybir.dt.float32, mybir.dt.uint16
+ACT = mybir.ActivationFunctionType
+ALU = mybir.AluOpType
+
+
+def tile_gaussian_kernel(tc, emb, base, offs, out):
+    nc = tc.nc
+    with (
+        tc.tile_pool(name="held", bufs=1) as held,
+        tc.psum_pool(name="psum", bufs=1) as psum,
+    ):
+        offsets = held.tile([N, N // 16], U16, name="offsets")
+        nc.sync.dma_start(offsets[:], offs)
+        nodes = held.tile([F, N], BF16, name="nodes")
+        nc.scalar.dma_start(nodes[:], emb)
+        window = held.tile([N, S], F32, name="window")
+        nc.sync.dma_start(window[:], base)
+
+        neg_mean_weights = held.tile([F, N], BF16, name="neg_mean_weights")
+        nc.vector.memset(neg_mean_weights[:], -1.0 / COUNT)
+        neg_half = held.tile([F, N], F32, name="neg_half")
+        nc.gpsimd.memset(neg_half[:], -0.5)
+        var_weights = held.tile([F, N], F32, name="var_weights")
+        nc.gpsimd.memset(var_weights[:], F / (COUNT - 1))
+
+        neg_col_means = psum.tile([N, N], F32, name="neg_col_means")
+        nc.tensor.matmul(neg_col_means[:], neg_mean_weights[:], nodes[:], start=True, stop=True)
+        neg_mu = held.tile([F, 1], F32, name="neg_mu")
+        nc.vector.reduce_sum(neg_mu[:], neg_col_means[:], axis=mybir.AxisListType.X)
+        deviations_sq = held.tile([F, N], F32, name="deviations_sq")
+        deviations_sq_sum = held.tile([F, 1], F32, name="deviations_sq_sum")
+        nc.scalar.activation(
+            deviations_sq[:], nodes[:], ACT.Square, bias=neg_mu[:], accum_out=deviations_sq_sum[:]
+        )
+        f_var = psum.tile([N, 1], F32, name="f_var")
+        nc.tensor.matmul(f_var[:], var_weights[:], deviations_sq_sum[:], start=True, stop=True)
+        inv_f_var = held.tile([N, 1], F32, name="inv_f_var")
+        nc.vector.reciprocal(inv_f_var[:], f_var[:])
+
+        squares = held.tile([F, N], F32, name="squares")
+        nc.vector.tensor_tensor(squares[:], nodes[:], nodes[:], ALU.mult)
+        neg_half_dist = psum.tile([N, N], F32, name="neg_half_dist")
+        nc.tensor.matmul(neg_half_dist[:], nodes[:], nodes[:], start=True, stop=False)
+        nc.tensor.matmul(neg_half_dist[:], neg_half[:], squares[:], start=False, stop=False)
+        nc.tensor.matmul(neg_half_dist[:], squares[:], neg_half[:], start=False, stop=True)
+
+        clamped = held.tile([N, N], F32, name="clamped")
+        nc.vector.tensor_scalar_min(clamped[:], neg_half_dist[:], 0.0)
+        affinity = held.tile([N, N], F32, name="affinity")
+        nc.scalar.activation(affinity[:], clamped[:], ACT.Exp, scale=inv_f_var[:])
+        nc.scalar.activation(window[:].indirect(offsets[:]), affinity[:], ACT.Copy)
+        nc.sync.dma_start(out, window[:])

@@ -25,6 +25,10 @@ def tile_gaussian_kernel(tc, emb, base, offs, out):
         window = held.tile([N, S], F32, name="window")
         nc.sync.dma_start(window[:], base)
 
+        warm = held.tile([N, 1], F32, name="warm")
+        nc.vector.memset(warm[:], 0.0)
+        nc.scalar.activation(warm[:], warm[:], ACT.Exp)
+
         neg_mean_weights = held.tile([F, N], BF16, name="neg_mean_weights")
         nc.vector.memset(neg_mean_weights[:], -1.0 / COUNT)
         neg_half = held.tile([F, N], F32, name="neg_half")

@@ -54,11 +54,12 @@ def tile_gaussian_kernel(tc, emb, base, offs, out):
         nc.vector.tensor_tensor(squares[:], nodes[:], nodes[:], ALU.mult)
         neg_half_dist = psum.tile([N, N], F32, name="neg_half_dist")
         nc.tensor.matmul(neg_half_dist[:], nodes[:], nodes[:], start=True, stop=False)
-        nc.tensor.matmul(neg_half_dist[:], neg_half[:], squares[:], start=False, stop=False)
-        nc.tensor.matmul(neg_half_dist[:], squares[:], neg_half[:], start=False, stop=True)
+        nc.tensor.matmul(neg_half_dist[:], neg_half[:], squares[:], start=False, stop=True)
+        neg_half_sq = psum.tile([N, 1], F32, name="neg_half_sq")
+        nc.tensor.matmul(neg_half_sq[:], squares[:], neg_half[:, 0:1], start=True, stop=True)
 
         clamped = held.tile([N, N], F32, name="clamped")
-        nc.vector.tensor_scalar_min(clamped[:], neg_half_dist[:], 0.0)
+        nc.vector.tensor_scalar(clamped[:], neg_half_dist[:], neg_half_sq[:], 0.0, ALU.add, ALU.min)
         affinity = held.tile([N, N], F32, name="affinity")
         nc.scalar.activation(affinity[:], clamped[:], ACT.Exp, scale=inv_f_var[:])
         nc.scalar.activation(window[:].indirect(offsets[:]), affinity[:], ACT.Copy)

@@ -10,6 +10,7 @@ FLOPS = 2 * F * N * N
 BF16, F32, U16 = mybir.dt.bfloat16, mybir.dt.float32, mybir.dt.uint16
 ACT = mybir.ActivationFunctionType
 ALU = mybir.AluOpType
+X = mybir.AxisListType.X
 
 
 def tile_gaussian_kernel(tc, emb, base, offs, out):
@@ -36,25 +37,29 @@ def tile_gaussian_kernel(tc, emb, base, offs, out):
         var_weights = held.tile([F, N], F32, name="var_weights")
         nc.gpsimd.memset(var_weights[:], F / (COUNT - 1))
 
-        neg_col_means = psum.tile([N, N], F32, name="neg_col_means")
-        nc.tensor.matmul(neg_col_means[:], neg_mean_weights[:], nodes[:], start=True, stop=True)
-        neg_mu = held.tile([F, 1], F32, name="neg_mu")
-        nc.vector.reduce_sum(neg_mu[:], neg_col_means[:], axis=mybir.AxisListType.X)
-        deviations_sq = held.tile([F, N], F32, name="deviations_sq")
-        deviations_sq_sum = held.tile([F, 1], F32, name="deviations_sq_sum")
-        nc.scalar.activation(
-            deviations_sq[:], nodes[:], ACT.Square, bias=neg_mu[:], accum_out=deviations_sq_sum[:]
-        )
-        f_var = psum.tile([N, 1], F32, name="f_var")
-        nc.tensor.matmul(f_var[:], var_weights[:], deviations_sq_sum[:], start=True, stop=True)
-        inv_f_var = held.tile([N, 1], F32, name="inv_f_var")
-        nc.vector.reciprocal(inv_f_var[:], f_var[:])
-
         squares = held.tile([F, N], F32, name="squares")
         nc.vector.tensor_tensor(squares[:], nodes[:], nodes[:], ALU.mult)
+        row_sq = held.tile([F, 1], F32, name="row_sq")
+        nc.vector.reduce_sum(row_sq[:], squares[:], axis=X)
+
+        neg_col_means = psum.tile([N, N], F32, name="neg_col_means")
+        nc.tensor.matmul(neg_col_means[:], neg_mean_weights[:], nodes[:], start=True, stop=True)
+        neg_mu = held.tile([N, 1], F32, name="neg_mu")
+        nc.vector.reduce_sum(neg_mu[:], neg_col_means[:], axis=X)
+        scaled_mu = held.tile([N, 1], F32, name="scaled_mu")
+        nc.vector.tensor_scalar_mul(scaled_mu[:], neg_mu[:], -F * COUNT / (COUNT - 1))
+
         neg_half_dist = psum.tile([N, N], F32, name="neg_half_dist")
         nc.tensor.matmul(neg_half_dist[:], nodes[:], nodes[:], start=True, stop=False)
         nc.tensor.matmul(neg_half_dist[:], neg_half[:], squares[:], start=False, stop=True)
+
+        f_sum_sq = psum.tile([N, 1], F32, name="f_sum_sq")
+        nc.tensor.matmul(f_sum_sq[:], var_weights[:], row_sq[:], start=True, stop=True)
+        f_var = held.tile([N, 1], F32, name="f_var")
+        nc.vector.tensor_scalar(f_var[:], neg_mu[:], scaled_mu[:], f_sum_sq[:], ALU.mult, ALU.add)
+        inv_f_var = held.tile([N, 1], F32, name="inv_f_var")
+        nc.vector.reciprocal(inv_f_var[:], f_var[:])
+
         neg_half_sq = psum.tile([N, 1], F32, name="neg_half_sq")
         nc.tensor.matmul(neg_half_sq[:], squares[:], neg_half[:, 0:1], start=True, stop=True)
 

@@ -10,7 +10,6 @@ FLOPS = 2 * F * N * N
 BF16, F32, U16 = mybir.dt.bfloat16, mybir.dt.float32, mybir.dt.uint16
 ACT = mybir.ActivationFunctionType
 ALU = mybir.AluOpType
-X = mybir.AxisListType.X
 
 
 def tile_gaussian_kernel(tc, emb, base, offs, out):
@@ -19,10 +18,10 @@ def tile_gaussian_kernel(tc, emb, base, offs, out):
         tc.tile_pool(name="held", bufs=1) as held,
         tc.psum_pool(name="psum", bufs=1) as psum,
     ):
+        nodes = held.tile([F, N], BF16, name="nodes")
+        nc.sync.dma_start(nodes[:], emb)
         offsets = held.tile([N, N // 16], U16, name="offsets")
         nc.sync.dma_start(offsets[:], offs)
-        nodes = held.tile([F, N], BF16, name="nodes")
-        nc.scalar.dma_start(nodes[:], emb)
         window = held.tile([N, S], F32, name="window")
         nc.sync.dma_start(window[:], base)
 
@@ -37,34 +36,29 @@ def tile_gaussian_kernel(tc, emb, base, offs, out):
         var_weights = held.tile([F, N], F32, name="var_weights")
         nc.gpsimd.memset(var_weights[:], F / (COUNT - 1))
 
-        squares = held.tile([F, N], F32, name="squares")
-        nc.vector.tensor_tensor(squares[:], nodes[:], nodes[:], ALU.mult)
-        row_sq = held.tile([F, 1], F32, name="row_sq")
-        nc.vector.reduce_sum(row_sq[:], squares[:], axis=X)
-
         neg_col_means = psum.tile([N, N], F32, name="neg_col_means")
         nc.tensor.matmul(neg_col_means[:], neg_mean_weights[:], nodes[:], start=True, stop=True)
-        neg_mu = held.tile([N, 1], F32, name="neg_mu")
-        nc.vector.reduce_sum(neg_mu[:], neg_col_means[:], axis=X)
-        scaled_mu = held.tile([N, 1], F32, name="scaled_mu")
-        nc.vector.tensor_scalar_mul(scaled_mu[:], neg_mu[:], -F * COUNT / (COUNT - 1))
-
-        neg_half_dist = psum.tile([N, N], F32, name="neg_half_dist")
-        nc.tensor.matmul(neg_half_dist[:], nodes[:], nodes[:], start=True, stop=False)
-        nc.tensor.matmul(neg_half_dist[:], neg_half[:], squares[:], start=False, stop=True)
-
-        f_sum_sq = psum.tile([N, 1], F32, name="f_sum_sq")
-        nc.tensor.matmul(f_sum_sq[:], var_weights[:], row_sq[:], start=True, stop=True)
-        f_var = held.tile([N, 1], F32, name="f_var")
-        nc.vector.tensor_scalar(f_var[:], neg_mu[:], scaled_mu[:], f_sum_sq[:], ALU.mult, ALU.add)
+        neg_mu = held.tile([F, 1], F32, name="neg_mu")
+        nc.vector.reduce_sum(neg_mu[:], neg_col_means[:], axis=mybir.AxisListType.X)
+        deviations_sq = held.tile([F, N], F32, name="deviations_sq")
+        deviations_sq_sum = held.tile([F, 1], F32, name="deviations_sq_sum")
+        nc.scalar.activation(
+            deviations_sq[:], nodes[:], ACT.Square, bias=neg_mu[:], accum_out=deviations_sq_sum[:]
+        )
+        f_var = psum.tile([N, 1], F32, name="f_var")
+        nc.tensor.matmul(f_var[:], var_weights[:], deviations_sq_sum[:], start=True, stop=True)
         inv_f_var = held.tile([N, 1], F32, name="inv_f_var")
         nc.vector.reciprocal(inv_f_var[:], f_var[:])
 
-        neg_half_sq = psum.tile([N, 1], F32, name="neg_half_sq")
-        nc.tensor.matmul(neg_half_sq[:], squares[:], neg_half[:, 0:1], start=True, stop=True)
+        squares = held.tile([F, N], F32, name="squares")
+        nc.vector.tensor_tensor(squares[:], nodes[:], nodes[:], ALU.mult)
+        neg_half_dist = psum.tile([N, N], F32, name="neg_half_dist")
+        nc.tensor.matmul(neg_half_dist[:], nodes[:], nodes[:], start=True, stop=False)
+        nc.tensor.matmul(neg_half_dist[:], neg_half[:], squares[:], start=False, stop=False)
+        nc.tensor.matmul(neg_half_dist[:], squares[:], neg_half[:], start=False, stop=True)
 
         clamped = held.tile([N, N], F32, name="clamped")
-        nc.vector.tensor_scalar(clamped[:], neg_half_dist[:], neg_half_sq[:], 0.0, ALU.add, ALU.min)
+        nc.vector.tensor_scalar_min(clamped[:], neg_half_dist[:], 0.0)
         affinity = held.tile([N, N], F32, name="affinity")
         nc.scalar.activation(affinity[:], clamped[:], ACT.Exp, scale=inv_f_var[:])
         nc.scalar.activation(window[:].indirect(offsets[:]), affinity[:], ACT.Copy)

@@ -4,6 +4,7 @@ F = 128
 N = 128
 S = 256
 COUNT = F * N
+WARM_MATMULS = 14
 
 FLOPS = 2 * F * N * N
 
@@ -18,6 +19,12 @@ def tile_gaussian_kernel(tc, emb, base, offs, out):
         tc.tile_pool(name="held", bufs=1) as held,
         tc.psum_pool(name="psum", bufs=1) as psum,
     ):
+        neg_mean_weights = held.tile([F, N], BF16, name="neg_mean_weights")
+        nc.gpsimd.memset(neg_mean_weights[:], -1.0 / COUNT)
+        warm_bank = psum.tile([N, N], F32, name="warm_bank")
+        for i in range(WARM_MATMULS):
+            nc.tensor.matmul(warm_bank[:], neg_mean_weights[:], neg_mean_weights[:], start=True, stop=True)
+
         nodes = held.tile([F, N], BF16, name="nodes")
         nc.sync.dma_start(nodes[:], emb)
         offsets = held.tile([N, N // 16], U16, name="offsets")
@@ -29,8 +36,6 @@ def tile_gaussian_kernel(tc, emb, base, offs, out):
         nc.vector.memset(warm[:], 0.0)
         nc.scalar.activation(warm[:], warm[:], ACT.Exp)
 
-        neg_mean_weights = held.tile([F, N], BF16, name="neg_mean_weights")
-        nc.vector.memset(neg_mean_weights[:], -1.0 / COUNT)
         neg_half = held.tile([F, N], F32, name="neg_half")
         nc.gpsimd.memset(neg_half[:], -0.5)
         var_weights = held.tile([F, N], F32, name="var_weights")

@@ -4,7 +4,6 @@ F = 128
 N = 128
 S = 256
 COUNT = F * N
-WARM_MATMULS = 14
 
 FLOPS = 2 * F * N * N
 
@@ -19,12 +18,6 @@ def tile_gaussian_kernel(tc, emb, base, offs, out):
         tc.tile_pool(name="held", bufs=1) as held,
         tc.psum_pool(name="psum", bufs=1) as psum,
     ):
-        neg_mean_weights = held.tile([F, N], BF16, name="neg_mean_weights")
-        nc.gpsimd.memset(neg_mean_weights[:], -1.0 / COUNT)
-        warm_bank = psum.tile([N, N], F32, name="warm_bank")
-        for i in range(WARM_MATMULS):
-            nc.tensor.matmul(warm_bank[:], neg_mean_weights[:], neg_mean_weights[:], start=True, stop=True)
-
         nodes = held.tile([F, N], BF16, name="nodes")
         nc.sync.dma_start(nodes[:], emb)
         offsets = held.tile([N, N // 16], U16, name="offsets")
@@ -36,7 +29,9 @@ def tile_gaussian_kernel(tc, emb, base, offs, out):
         nc.vector.memset(warm[:], 0.0)
         nc.scalar.activation(warm[:], warm[:], ACT.Exp)
 
-        neg_half = held.tile([F, N], F32, name="neg_half")
+        neg_mean_weights = held.tile([F, N], BF16, name="neg_mean_weights")
+        nc.vector.memset(neg_mean_weights[:], -1.0 / COUNT)
+        neg_half = held.tile([F, N], BF16, name="neg_half")
         nc.gpsimd.memset(neg_half[:], -0.5)
         var_weights = held.tile([F, N], F32, name="var_weights")
         nc.gpsimd.memset(var_weights[:], F / (COUNT - 1))
@@ -55,12 +50,18 @@ def tile_gaussian_kernel(tc, emb, base, offs, out):
         inv_f_var = held.tile([N, 1], F32, name="inv_f_var")
         nc.vector.reciprocal(inv_f_var[:], f_var[:])
 
+        squares_hi = held.tile([F, N], BF16, name="squares_hi")
+        nc.vector.tensor_tensor(squares_hi[:], nodes[:], nodes[:], ALU.mult)
         squares = held.tile([F, N], F32, name="squares")
         nc.vector.tensor_tensor(squares[:], nodes[:], nodes[:], ALU.mult)
+        squares_lo = held.tile([F, N], BF16, name="squares_lo")
+        nc.vector.tensor_tensor(squares_lo[:], squares[:], squares_hi[:], ALU.subtract)
         neg_half_dist = psum.tile([N, N], F32, name="neg_half_dist")
         nc.tensor.matmul(neg_half_dist[:], nodes[:], nodes[:], start=True, stop=False)
-        nc.tensor.matmul(neg_half_dist[:], neg_half[:], squares[:], start=False, stop=False)
-        nc.tensor.matmul(neg_half_dist[:], squares[:], neg_half[:], start=False, stop=True)
+        nc.tensor.matmul(neg_half_dist[:], neg_half[:], squares_hi[:], start=False, stop=False)
+        nc.tensor.matmul(neg_half_dist[:], squares_hi[:], neg_half[:], start=False, stop=False)
+        nc.tensor.matmul(neg_half_dist[:], neg_half[:], squares_lo[:], start=False, stop=False)
+        nc.tensor.matmul(neg_half_dist[:], squares_lo[:], neg_half[:], start=False, stop=True)
 
         clamped = held.tile([N, N], F32, name="clamped")
         nc.vector.tensor_scalar_min(clamped[:], neg_half_dist[:], 0.0)

@@ -4,6 +4,9 @@ F = 128
 N = 128
 S = 256
 COUNT = F * N
+SHIFT_COLS = 16
+
+UNBIAS = (COUNT - 1) / (COUNT * F)
 
 FLOPS = 2 * F * N * N
 
@@ -20,6 +23,8 @@ def tile_gaussian_kernel(tc, emb, base, offs, out):
     ):
         nodes = held.tile([F, N], BF16, name="nodes")
         nc.sync.dma_start(nodes[:], emb)
+        shift = held.tile([F, SHIFT_COLS], BF16, name="shift")
+        nc.sync.dma_start(shift[:], emb[0, 0:SHIFT_COLS].partition_broadcast(F))
         offsets = held.tile([N, N // 16], U16, name="offsets")
         nc.sync.dma_start(offsets[:], offs)
         window = held.tile([N, S], F32, name="window")
@@ -29,26 +34,30 @@ def tile_gaussian_kernel(tc, emb, base, offs, out):
         nc.vector.memset(warm[:], 0.0)
         nc.scalar.activation(warm[:], warm[:], ACT.Exp)
 
-        neg_mean_weights = held.tile([F, N], BF16, name="neg_mean_weights")
-        nc.vector.memset(neg_mean_weights[:], -1.0 / COUNT)
         neg_half = held.tile([F, N], BF16, name="neg_half")
         nc.gpsimd.memset(neg_half[:], -0.5)
-        var_weights = held.tile([F, N], F32, name="var_weights")
-        nc.gpsimd.memset(var_weights[:], F / (COUNT - 1))
+        mean_weights = held.tile([F, N], F32, name="mean_weights")
+        nc.gpsimd.memset(mean_weights[:], 1.0 / COUNT)
 
-        neg_col_means = psum.tile([N, N], F32, name="neg_col_means")
-        nc.tensor.matmul(neg_col_means[:], neg_mean_weights[:], nodes[:], start=True, stop=True)
-        neg_mu = held.tile([F, 1], F32, name="neg_mu")
-        nc.vector.reduce_sum(neg_mu[:], neg_col_means[:], axis=mybir.AxisListType.X)
-        deviations_sq = held.tile([F, N], F32, name="deviations_sq")
-        deviations_sq_sum = held.tile([F, 1], F32, name="deviations_sq_sum")
+        partial_sums = held.tile([F, 2], F32, name="partial_sums")
+        shifted_sq = held.tile([F, N], F32, name="shifted_sq")
         nc.scalar.activation(
-            deviations_sq[:], nodes[:], ACT.Square, bias=neg_mu[:], accum_out=deviations_sq_sum[:]
+            shifted_sq[:], nodes[:], ACT.Square, bias=shift[:, 0:1], scale=-1.0,
+            accum_out=partial_sums[:, 0:1],
         )
-        f_var = psum.tile([N, 1], F32, name="f_var")
-        nc.tensor.matmul(f_var[:], var_weights[:], deviations_sq_sum[:], start=True, stop=True)
-        inv_f_var = held.tile([N, 1], F32, name="inv_f_var")
-        nc.vector.reciprocal(inv_f_var[:], f_var[:])
+        shifted = held.tile([F, N], F32, name="shifted")
+        nc.vector.tensor_scalar(
+            shifted[:], nodes[:], shift[:, 0:1], None, ALU.subtract, ALU.add,
+            accum_out=partial_sums[:, 1:2],
+        )
+        means = psum.tile([N, 2], F32, name="means")
+        nc.tensor.matmul(means[:], mean_weights[:], partial_sums[:], start=True, stop=True)
+        neg_variance = held.tile([N, 1], F32, name="neg_variance")
+        nc.vector.tensor_scalar(
+            neg_variance[:], means[:, 1:2], means[:, 1:2], means[:, 0:1], ALU.mult, ALU.subtract
+        )
+        neg_inv_variance = held.tile([N, 1], F32, name="neg_inv_variance")
+        nc.vector.reciprocal(neg_inv_variance[:], neg_variance[:])
 
         squares_hi = held.tile([F, N], BF16, name="squares_hi")
         nc.vector.tensor_tensor(squares_hi[:], nodes[:], nodes[:], ALU.mult)
@@ -64,8 +73,8 @@ def tile_gaussian_kernel(tc, emb, base, offs, out):
         nc.tensor.matmul(neg_half_dist[:], squares_lo[:], neg_half[:], start=False, stop=True)
 
         clamped = held.tile([N, N], F32, name="clamped")
-        nc.vector.tensor_scalar_min(clamped[:], neg_half_dist[:], 0.0)
+        nc.vector.tensor_scalar(clamped[:], neg_half_dist[:], 0.0, -UNBIAS, ALU.min, ALU.mult)
         affinity = held.tile([N, N], F32, name="affinity")
-        nc.scalar.activation(affinity[:], clamped[:], ACT.Exp, scale=inv_f_var[:])
+        nc.scalar.activation(affinity[:], clamped[:], ACT.Exp, scale=neg_inv_variance[:])
         nc.scalar.activation(window[:].indirect(offsets[:]), affinity[:], ACT.Copy)
         nc.sync.dma_start(out, window[:])

@@ -4,7 +4,6 @@ F = 128
 N = 128
 S = 256
 COUNT = F * N
-SHIFT_COLS = 16
 
 UNBIAS = (COUNT - 1) / (COUNT * F)
 
@@ -23,8 +22,6 @@ def tile_gaussian_kernel(tc, emb, base, offs, out):
     ):
         nodes = held.tile([F, N], BF16, name="nodes")
         nc.sync.dma_start(nodes[:], emb)
-        shift = held.tile([F, SHIFT_COLS], BF16, name="shift")
-        nc.sync.dma_start(shift[:], emb[0, 0:SHIFT_COLS].partition_broadcast(F))
         offsets = held.tile([N, N // 16], U16, name="offsets")
         nc.sync.dma_start(offsets[:], offs)
         window = held.tile([N, S], F32, name="window")
@@ -40,16 +37,9 @@ def tile_gaussian_kernel(tc, emb, base, offs, out):
         nc.gpsimd.memset(mean_weights[:], 1.0 / COUNT)
 
         partial_sums = held.tile([F, 2], F32, name="partial_sums")
-        shifted_sq = held.tile([F, N], F32, name="shifted_sq")
-        nc.scalar.activation(
-            shifted_sq[:], nodes[:], ACT.Square, bias=shift[:, 0:1], scale=-1.0,
-            accum_out=partial_sums[:, 0:1],
-        )
-        shifted = held.tile([F, N], F32, name="shifted")
-        nc.vector.tensor_scalar(
-            shifted[:], nodes[:], shift[:, 0:1], None, ALU.subtract, ALU.add,
-            accum_out=partial_sums[:, 1:2],
-        )
+        squares = held.tile([F, N], F32, name="squares")
+        nc.scalar.activation(squares[:], nodes[:], ACT.Square, accum_out=partial_sums[:, 0:1])
+        nc.vector.reduce_sum(partial_sums[:, 1:2], nodes[:], axis=mybir.AxisListType.X)
         means = psum.tile([N, 2], F32, name="means")
         nc.tensor.matmul(means[:], mean_weights[:], partial_sums[:], start=True, stop=True)
         neg_variance = held.tile([N, 1], F32, name="neg_variance")
@@ -61,8 +51,6 @@ def tile_gaussian_kernel(tc, emb, base, offs, out):
 
         squares_hi = held.tile([F, N], BF16, name="squares_hi")
         nc.vector.tensor_tensor(squares_hi[:], nodes[:], nodes[:], ALU.mult)
-        squares = held.tile([F, N], F32, name="squares")
-        nc.vector.tensor_tensor(squares[:], nodes[:], nodes[:], ALU.mult)
         squares_lo = held.tile([F, N], BF16, name="squares_lo")
         nc.vector.tensor_tensor(squares_lo[:], squares[:], squares_hi[:], ALU.subtract)
         neg_half_dist = psum.tile([N, N], F32, name="neg_half_dist")

@@ -39,26 +39,29 @@ def tile_gaussian_kernel(tc, emb, base, offs, out):
         partial_sums = held.tile([F, 2], F32, name="partial_sums")
         squares = held.tile([F, N], F32, name="squares")
         nc.scalar.activation(squares[:], nodes[:], ACT.Square, accum_out=partial_sums[:, 0:1])
+
+        squares_hi = held.tile([F, N], BF16, name="squares_hi")
+        nc.vector.tensor_tensor(squares_hi[:], nodes[:], nodes[:], ALU.mult)
         nc.vector.reduce_sum(partial_sums[:, 1:2], nodes[:], axis=mybir.AxisListType.X)
+        neg_half_dist = psum.tile([N, N], F32, name="neg_half_dist")
+        nc.tensor.matmul(neg_half_dist[:], nodes[:], nodes[:], start=True, stop=False)
+        nc.tensor.matmul(neg_half_dist[:], neg_half[:], squares_hi[:], start=False, stop=False)
+        nc.tensor.matmul(neg_half_dist[:], squares_hi[:], neg_half[:], start=False, stop=False)
+        squares_lo = held.tile([F, N], BF16, name="squares_lo")
+        nc.vector.tensor_tensor(squares_lo[:], squares[:], squares_hi[:], ALU.subtract)
+
         means = psum.tile([N, 2], F32, name="means")
         nc.tensor.matmul(means[:], mean_weights[:], partial_sums[:], start=True, stop=True)
+
+        nc.tensor.matmul(neg_half_dist[:], neg_half[:], squares_lo[:], start=False, stop=False)
+        nc.tensor.matmul(neg_half_dist[:], squares_lo[:], neg_half[:], start=False, stop=True)
+
         neg_variance = held.tile([N, 1], F32, name="neg_variance")
         nc.vector.tensor_scalar(
             neg_variance[:], means[:, 1:2], means[:, 1:2], means[:, 0:1], ALU.mult, ALU.subtract
         )
         neg_inv_variance = held.tile([N, 1], F32, name="neg_inv_variance")
         nc.vector.reciprocal(neg_inv_variance[:], neg_variance[:])
-
-        squares_hi = held.tile([F, N], BF16, name="squares_hi")
-        nc.vector.tensor_tensor(squares_hi[:], nodes[:], nodes[:], ALU.mult)
-        squares_lo = held.tile([F, N], BF16, name="squares_lo")
-        nc.vector.tensor_tensor(squares_lo[:], squares[:], squares_hi[:], ALU.subtract)
-        neg_half_dist = psum.tile([N, N], F32, name="neg_half_dist")
-        nc.tensor.matmul(neg_half_dist[:], nodes[:], nodes[:], start=True, stop=False)
-        nc.tensor.matmul(neg_half_dist[:], neg_half[:], squares_hi[:], start=False, stop=False)
-        nc.tensor.matmul(neg_half_dist[:], squares_hi[:], neg_half[:], start=False, stop=False)
-        nc.tensor.matmul(neg_half_dist[:], neg_half[:], squares_lo[:], start=False, stop=False)
-        nc.tensor.matmul(neg_half_dist[:], squares_lo[:], neg_half[:], start=False, stop=True)
 
         clamped = held.tile([N, N], F32, name="clamped")
         nc.vector.tensor_scalar(clamped[:], neg_half_dist[:], 0.0, -UNBIAS, ALU.min, ALU.mult)

@@ -35,31 +35,33 @@ def tile_gaussian_kernel(tc, emb, base, offs, out):
         nc.gpsimd.memset(neg_half[:], -0.5)
         mean_weights = held.tile([F, N], F32, name="mean_weights")
         nc.gpsimd.memset(mean_weights[:], 1.0 / COUNT)
+        mean_weights_bf = held.tile([F, N], BF16, name="mean_weights_bf")
+        nc.gpsimd.memset(mean_weights_bf[:], 1.0 / COUNT)
 
-        partial_sums = held.tile([F, 2], F32, name="partial_sums")
         squares = held.tile([F, N], F32, name="squares")
-        nc.scalar.activation(squares[:], nodes[:], ACT.Square, accum_out=partial_sums[:, 0:1])
-
+        sq_sums = held.tile([F, 1], F32, name="sq_sums")
+        nc.scalar.activation(squares[:], nodes[:], ACT.Square, accum_out=sq_sums[:])
         squares_hi = held.tile([F, N], BF16, name="squares_hi")
         nc.vector.tensor_tensor(squares_hi[:], nodes[:], nodes[:], ALU.mult)
-        nc.vector.reduce_sum(partial_sums[:, 1:2], nodes[:], axis=mybir.AxisListType.X)
+
+        col_means = psum.tile([N, N], F32, name="col_means")
+        nc.tensor.matmul(col_means[:], mean_weights_bf[:], nodes[:], start=True, stop=True)
+
         neg_half_dist = psum.tile([N, N], F32, name="neg_half_dist")
         nc.tensor.matmul(neg_half_dist[:], nodes[:], nodes[:], start=True, stop=False)
         nc.tensor.matmul(neg_half_dist[:], neg_half[:], squares_hi[:], start=False, stop=False)
         nc.tensor.matmul(neg_half_dist[:], squares_hi[:], neg_half[:], start=False, stop=False)
+        mean_sq = psum.tile([N, 1], F32, name="mean_sq")
+        nc.tensor.matmul(mean_sq[:], mean_weights[:], sq_sums[:], start=True, stop=True)
         squares_lo = held.tile([F, N], BF16, name="squares_lo")
         nc.vector.tensor_tensor(squares_lo[:], squares[:], squares_hi[:], ALU.subtract)
-
-        means = psum.tile([N, 2], F32, name="means")
-        nc.tensor.matmul(means[:], mean_weights[:], partial_sums[:], start=True, stop=True)
-
         nc.tensor.matmul(neg_half_dist[:], neg_half[:], squares_lo[:], start=False, stop=False)
         nc.tensor.matmul(neg_half_dist[:], squares_lo[:], neg_half[:], start=False, stop=True)
 
+        mu = held.tile([N, 1], F32, name="mu")
+        nc.vector.reduce_sum(mu[:], col_means[:], axis=mybir.AxisListType.X)
         neg_variance = held.tile([N, 1], F32, name="neg_variance")
-        nc.vector.tensor_scalar(
-            neg_variance[:], means[:, 1:2], means[:, 1:2], means[:, 0:1], ALU.mult, ALU.subtract
-        )
+        nc.vector.tensor_scalar(neg_variance[:], mu[:], mu[:], mean_sq[:], ALU.mult, ALU.subtract)
         neg_inv_variance = held.tile([N, 1], F32, name="neg_inv_variance")
         nc.vector.reciprocal(neg_inv_variance[:], neg_variance[:])
 

@@ -32,11 +32,11 @@ def tile_gaussian_kernel(tc, emb, base, offs, out):
         nc.scalar.activation(warm[:], warm[:], ACT.Exp)
 
         neg_half = held.tile([F, N], BF16, name="neg_half")
-        nc.gpsimd.memset(neg_half[:], -0.5)
+        nc.vector.memset(neg_half[:], -0.5)
         mean_weights = held.tile([F, N], F32, name="mean_weights")
-        nc.gpsimd.memset(mean_weights[:], 1.0 / COUNT)
+        nc.vector.memset(mean_weights[:], 1.0 / COUNT)
         mean_weights_bf = held.tile([F, N], BF16, name="mean_weights_bf")
-        nc.gpsimd.memset(mean_weights_bf[:], 1.0 / COUNT)
+        nc.vector.memset(mean_weights_bf[:], 1.0 / COUNT)
 
         squares = held.tile([F, N], F32, name="squares")
         sq_sums = held.tile([F, 1], F32, name="sq_sums")

@@ -5,7 +5,7 @@ N = 128
 S = 256
 COUNT = F * N
 
-UNBIAS = (COUNT - 1) / (COUNT * F)
+F_BESSEL = F * COUNT / (COUNT - 1)
 
 FLOPS = 2 * F * N * N
 
@@ -33,8 +33,8 @@ def tile_gaussian_kernel(tc, emb, base, offs, out):
 
         neg_half = held.tile([F, N], BF16, name="neg_half")
         nc.vector.memset(neg_half[:], -0.5)
-        mean_weights = held.tile([F, N], F32, name="mean_weights")
-        nc.vector.memset(mean_weights[:], 1.0 / COUNT)
+        f_var_weights = held.tile([F, N], F32, name="f_var_weights")
+        nc.vector.memset(f_var_weights[:], F_BESSEL / COUNT)
         mean_weights_bf = held.tile([F, N], BF16, name="mean_weights_bf")
         nc.vector.memset(mean_weights_bf[:], 1.0 / COUNT)
 
@@ -47,27 +47,32 @@ def tile_gaussian_kernel(tc, emb, base, offs, out):
         col_means = psum.tile([N, N], F32, name="col_means")
         nc.tensor.matmul(col_means[:], mean_weights_bf[:], nodes[:], start=True, stop=True)
 
-        neg_half_dist = psum.tile([N, N], F32, name="neg_half_dist")
-        nc.tensor.matmul(neg_half_dist[:], nodes[:], nodes[:], start=True, stop=False)
-        nc.tensor.matmul(neg_half_dist[:], neg_half[:], squares_hi[:], start=False, stop=False)
-        nc.tensor.matmul(neg_half_dist[:], squares_hi[:], neg_half[:], start=False, stop=False)
-        mean_sq = psum.tile([N, 1], F32, name="mean_sq")
-        nc.tensor.matmul(mean_sq[:], mean_weights[:], sq_sums[:], start=True, stop=True)
+        inner_less_row = psum.tile([N, N], F32, name="inner_less_row")
+        nc.tensor.matmul(inner_less_row[:], nodes[:], nodes[:], start=True, stop=False)
+        nc.tensor.matmul(inner_less_row[:], neg_half[:], squares_hi[:], start=False, stop=False)
+        neg_half_sq = psum.tile([N, 1], F32, name="neg_half_sq")
+        nc.tensor.matmul(neg_half_sq[:], squares_hi[:], neg_half[:, 0:1], start=True, stop=False)
+        sq_term = psum.tile([N, 1], F32, name="sq_term")
+        nc.tensor.matmul(sq_term[:], f_var_weights[:], sq_sums[:], start=True, stop=True)
         squares_lo = held.tile([F, N], BF16, name="squares_lo")
         nc.vector.tensor_tensor(squares_lo[:], squares[:], squares_hi[:], ALU.subtract)
-        nc.tensor.matmul(neg_half_dist[:], neg_half[:], squares_lo[:], start=False, stop=False)
-        nc.tensor.matmul(neg_half_dist[:], squares_lo[:], neg_half[:], start=False, stop=True)
+        nc.tensor.matmul(inner_less_row[:], neg_half[:], squares_lo[:], start=False, stop=True)
+        nc.tensor.matmul(neg_half_sq[:], squares_lo[:], neg_half[:, 0:1], start=False, stop=True)
 
         mu = held.tile([N, 1], F32, name="mu")
         nc.vector.reduce_sum(mu[:], col_means[:], axis=mybir.AxisListType.X)
-        neg_variance = held.tile([N, 1], F32, name="neg_variance")
-        nc.vector.tensor_scalar(neg_variance[:], mu[:], mu[:], mean_sq[:], ALU.mult, ALU.subtract)
-        neg_inv_variance = held.tile([N, 1], F32, name="neg_inv_variance")
-        nc.vector.reciprocal(neg_inv_variance[:], neg_variance[:])
+        mu_term = held.tile([N, 1], F32, name="mu_term")
+        nc.vector.tensor_scalar(mu_term[:], mu[:], mu[:], F_BESSEL, ALU.mult, ALU.mult)
+        f_var = held.tile([N, 1], F32, name="f_var")
+        nc.vector.tensor_scalar(f_var[:], sq_term[:], mu_term[:], None, ALU.subtract)
+        inv_f_var = held.tile([N, 1], F32, name="inv_f_var")
+        nc.vector.reciprocal(inv_f_var[:], f_var[:])
 
         clamped = held.tile([N, N], F32, name="clamped")
-        nc.vector.tensor_scalar(clamped[:], neg_half_dist[:], 0.0, -UNBIAS, ALU.min, ALU.mult)
+        nc.vector.tensor_scalar(
+            clamped[:], inner_less_row[:], neg_half_sq[:], 0.0, ALU.add, ALU.min
+        )
         affinity = held.tile([N, N], F32, name="affinity")
-        nc.scalar.activation(affinity[:], clamped[:], ACT.Exp, scale=neg_inv_variance[:])
+        nc.scalar.activation(affinity[:], clamped[:], ACT.Exp, scale=inv_f_var[:])
         nc.scalar.activation(window[:].indirect(offsets[:]), affinity[:], ACT.Copy)
         nc.sync.dma_start(out, window[:])

@@ -39,23 +39,25 @@ def tile_gaussian_kernel(tc, emb, base, offs, out):
         nc.vector.memset(mean_weights_bf[:], 1.0 / COUNT)
 
         squares = held.tile([F, N], F32, name="squares")
+        nc.vector.tensor_tensor(squares[:], nodes[:], nodes[:], ALU.mult)
+        squares_hi = squares[:].bitcast(BF16)[:, 1 : 2 * N : 2]
+
+        squares_again = held.tile([F, N], F32, name="squares_again")
         sq_sums = held.tile([F, 1], F32, name="sq_sums")
-        nc.scalar.activation(squares[:], nodes[:], ACT.Square, accum_out=sq_sums[:])
-        squares_hi = held.tile([F, N], BF16, name="squares_hi")
-        nc.vector.tensor_tensor(squares_hi[:], nodes[:], nodes[:], ALU.mult)
+        nc.scalar.activation(squares_again[:], nodes[:], ACT.Square, accum_out=sq_sums[:])
 
         col_means = psum.tile([N, N], F32, name="col_means")
         nc.tensor.matmul(col_means[:], mean_weights_bf[:], nodes[:], start=True, stop=True)
 
         inner_less_row = psum.tile([N, N], F32, name="inner_less_row")
         nc.tensor.matmul(inner_less_row[:], nodes[:], nodes[:], start=True, stop=False)
-        nc.tensor.matmul(inner_less_row[:], neg_half[:], squares_hi[:], start=False, stop=False)
+        nc.tensor.matmul(inner_less_row[:], neg_half[:], squares_hi, start=False, stop=False)
         neg_half_sq = psum.tile([N, 1], F32, name="neg_half_sq")
-        nc.tensor.matmul(neg_half_sq[:], squares_hi[:], neg_half[:, 0:1], start=True, stop=False)
+        nc.tensor.matmul(neg_half_sq[:], squares_hi, neg_half[:, 0:1], start=True, stop=False)
         sq_term = psum.tile([N, 1], F32, name="sq_term")
         nc.tensor.matmul(sq_term[:], f_var_weights[:], sq_sums[:], start=True, stop=True)
         squares_lo = held.tile([F, N], BF16, name="squares_lo")
-        nc.vector.tensor_tensor(squares_lo[:], squares[:], squares_hi[:], ALU.subtract)
+        nc.vector.tensor_tensor(squares_lo[:], squares[:], squares_hi, ALU.subtract)
         nc.tensor.matmul(inner_less_row[:], neg_half[:], squares_lo[:], start=False, stop=True)
         nc.tensor.matmul(neg_half_sq[:], squares_lo[:], neg_half[:, 0:1], start=False, stop=True)
 

@@ -39,12 +39,11 @@ def tile_gaussian_kernel(tc, emb, base, offs, out):
         nc.vector.memset(mean_weights_bf[:], 1.0 / COUNT)
 
         squares = held.tile([F, N], F32, name="squares")
-        nc.vector.tensor_tensor(squares[:], nodes[:], nodes[:], ALU.mult)
-        squares_hi = squares[:].bitcast(BF16)[:, 1 : 2 * N : 2]
-
-        squares_again = held.tile([F, N], F32, name="squares_again")
         sq_sums = held.tile([F, 1], F32, name="sq_sums")
-        nc.scalar.activation(squares_again[:], nodes[:], ACT.Square, accum_out=sq_sums[:])
+        nc.vector.scalar_tensor_tensor(
+            squares[:], nodes[:], 1.0, nodes[:], ALU.mult, ALU.mult, accum_out=sq_sums[:]
+        )
+        squares_hi = squares[:].bitcast(BF16)[:, 1 : 2 * N : 2]
 
         col_means = psum.tile([N, N], F32, name="col_means")
         nc.tensor.matmul(col_means[:], mean_weights_bf[:], nodes[:], start=True, stop=True)

@@ -45,8 +45,13 @@ def tile_gaussian_kernel(tc, emb, base, offs, out):
         )
         squares_hi = squares[:].bitcast(BF16)[:, 1 : 2 * N : 2]
 
-        col_means = psum.tile([N, N], F32, name="col_means")
-        nc.tensor.matmul(col_means[:], mean_weights_bf[:], nodes[:], start=True, stop=True)
+        col_means = psum.tile([N, N // 2], F32, name="col_means")
+        nc.tensor.matmul(
+            col_means[:], mean_weights_bf[:], nodes[:, 0 : N // 2], start=True, stop=False
+        )
+        nc.tensor.matmul(
+            col_means[:], mean_weights_bf[:], nodes[:, N // 2 : N], start=False, stop=True
+        )
 
         inner_less_row = psum.tile([N, N], F32, name="inner_less_row")
         nc.tensor.matmul(inner_less_row[:], nodes[:], nodes[:], start=True, stop=False)

import concourse.mybir as mybir

F = 128
N = 128
S = 256
COUNT = F * N

F_BESSEL = F * COUNT / (COUNT - 1)

FLOPS = 2 * F * N * N

BF16, F32, U16 = mybir.dt.bfloat16, mybir.dt.float32, mybir.dt.uint16
ACT = mybir.ActivationFunctionType
ALU = mybir.AluOpType


def tile_gaussian_kernel(tc, emb, base, offs, out):
    nc = tc.nc
    with (
        tc.tile_pool(name="held", bufs=1) as held,
        tc.psum_pool(name="psum", bufs=1) as psum,
    ):
        nodes = held.tile([F, N], BF16, name="nodes")
        nc.sync.dma_start(nodes[:], emb)
        offsets = held.tile([N, N // 16], U16, name="offsets")
        nc.sync.dma_start(offsets[:], offs)
        window = held.tile([N, S], F32, name="window")
        nc.sync.dma_start(window[:], base)

        warm = held.tile([N, 1], F32, name="warm")
        nc.vector.memset(warm[:], 0.0)
        nc.scalar.activation(warm[:], warm[:], ACT.Exp)

        neg_half = held.tile([F, N], BF16, name="neg_half")
        nc.vector.memset(neg_half[:], -0.5)
        f_var_weights = held.tile([F, N], F32, name="f_var_weights")
        nc.vector.memset(f_var_weights[:], F_BESSEL / COUNT)
        mean_weights_bf = held.tile([F, N], BF16, name="mean_weights_bf")
        nc.vector.memset(mean_weights_bf[:], 1.0 / COUNT)

        squares = held.tile([F, N], F32, name="squares")
        sq_sums = held.tile([F, 1], F32, name="sq_sums")
        nc.vector.scalar_tensor_tensor(
            squares[:], nodes[:], 1.0, nodes[:], ALU.mult, ALU.mult, accum_out=sq_sums[:]
        )
        squares_hi = squares[:].bitcast(BF16)[:, 1 : 2 * N : 2]

        col_means = psum.tile([N, N // 2], F32, name="col_means")
        nc.tensor.matmul(
            col_means[:], mean_weights_bf[:], nodes[:, 0 : N // 2], start=True, stop=False
        )
        nc.tensor.matmul(
            col_means[:], mean_weights_bf[:], nodes[:, N // 2 : N], start=False, stop=True
        )

        inner_less_row = psum.tile([N, N], F32, name="inner_less_row")
        nc.tensor.matmul(inner_less_row[:], nodes[:], nodes[:], start=True, stop=False)
        nc.tensor.matmul(inner_less_row[:], neg_half[:], squares_hi, start=False, stop=False)
        neg_half_sq = psum.tile([N, 1], F32, name="neg_half_sq")
        nc.tensor.matmul(neg_half_sq[:], squares_hi, neg_half[:, 0:1], start=True, stop=False)
        sq_term = psum.tile([N, 1], F32, name="sq_term")
        nc.tensor.matmul(sq_term[:], f_var_weights[:], sq_sums[:], start=True, stop=True)
        squares_lo = held.tile([F, N], BF16, name="squares_lo")
        nc.vector.tensor_tensor(squares_lo[:], squares[:], squares_hi, ALU.subtract)
        nc.tensor.matmul(inner_less_row[:], neg_half[:], squares_lo[:], start=False, stop=True)
        nc.tensor.matmul(neg_half_sq[:], squares_lo[:], neg_half[:, 0:1], start=False, stop=True)

        mu = held.tile([N, 1], F32, name="mu")
        nc.vector.reduce_sum(mu[:], col_means[:], axis=mybir.AxisListType.X)
        mu_term = held.tile([N, 1], F32, name="mu_term")
        nc.vector.tensor_scalar(mu_term[:], mu[:], mu[:], F_BESSEL, ALU.mult, ALU.mult)
        f_var = held.tile([N, 1], F32, name="f_var")
        nc.vector.tensor_scalar(f_var[:], sq_term[:], mu_term[:], None, ALU.subtract)
        inv_f_var = held.tile([N, 1], F32, name="inv_f_var")
        nc.vector.reciprocal(inv_f_var[:], f_var[:])

        clamped = held.tile([N, N], F32, name="clamped")
        nc.vector.tensor_scalar(
            clamped[:], inner_less_row[:], neg_half_sq[:], 0.0, ALU.add, ALU.min
        )
        affinity = held.tile([N, N], F32, name="affinity")
        nc.scalar.activation(affinity[:], clamped[:], ACT.Exp, scale=inv_f_var[:])
        nc.scalar.activation(window[:].indirect(offsets[:]), affinity[:], ACT.Copy)
        nc.sync.dma_start(out, window[:])
